import numpy as np
import ml_dtypes


def mxq(x, axis, fmt="e4m3"):
    dtype, down = {"e4m3": (ml_dtypes.float8_e4m3fn, 7), "e5m2": (ml_dtypes.float8_e5m2, 14)}[fmt]
    v = np.moveaxis(np.asarray(x, np.float32).astype(ml_dtypes.bfloat16).astype(np.float64), axis, -1)
    blocks = v.reshape(v.shape[:-1] + (-1, 32))
    amax = np.abs(blocks).max(-1, keepdims=True)
    byte = np.maximum(np.where(amax > 0, np.frexp(amax)[1] - 1 + 127, 0) - down, 1)
    scale = np.exp2(byte - 127.0)
    codes = (blocks / scale).astype(np.float32).astype(dtype).astype(np.float64)
    return np.moveaxis((codes * scale).reshape(v.shape), -1, axis)


WIDE = False


def mx_kscale(k):
    if not WIDE:
        return np.ones(k)
    levels = np.array([10, -10, 5, -5, 0])
    a = np.random.permutation(np.resize(levels, k // 512 * 4)).reshape(k // 512, 4)
    idx = np.arange(k)
    return np.exp2(a[idx // 512, idx % 128 // 32])


BF16 = ml_dtypes.bfloat16


def bf(x):
    return np.asarray(x, np.float32).astype(BF16)


def f64(x):
    return np.asarray(x).astype(np.float64)


E2M1 = np.array([0.0, 0.5, 1.0, 1.5, 2.0, 3.0, 4.0, 6.0, -0.0, -0.5, -1.0, -1.5, -2.0, -3.0, -4.0, -6.0])


def pack_weight(w, fmt):
    k, n = w.shape
    w = f64(bf(w)).reshape(k // 32, 32, n)
    amax = np.abs(w).max(1)
    if fmt == "e4m3":
        byte = np.frexp(amax)[1] - 1 + 127 - 7
    else:
        mant, ex = np.frexp(amax / 6.0)
        byte = np.where(mant > 0.5, ex, ex - 1) + 127
    byte = np.clip(np.where(amax > 0, byte, 1), 1, 254)
    scaled = (w * np.exp2(127.0 - byte)[:, None, :]).reshape(k, n).astype(np.float32)
    by_word = np.ascontiguousarray(scaled.reshape(k // 512, 128, 4, n).transpose(0, 1, 3, 2))
    if fmt == "e4m3":
        words = by_word.astype(ml_dtypes.float8_e4m3fn).view(np.uint8)
    else:
        c = by_word.astype(ml_dtypes.float4_e2m1fn).view(np.uint8) & 0xF
        words = c[..., 0::2] | (c[..., 1::2] << 4)
    return np.ascontiguousarray(words), np.ascontiguousarray(byte.astype(np.uint8).reshape(k // 512, 16, n))


def unpack_weight(words, scales, fmt):
    g, p, n, _ = words.shape
    if fmt == "e4m3":
        vals = np.ascontiguousarray(words).view(ml_dtypes.float8_e4m3fn).astype(np.float64)
    else:
        nib = np.empty((g, p, n, 4), np.uint8)
        nib[..., 0::2] = words & 0xF
        nib[..., 1::2] = words >> 4
        vals = E2M1[nib]
    vals = vals * np.repeat(np.exp2(scales.astype(np.float64) - 127.0), 8, axis=1)[..., None]
    return vals.transpose(0, 1, 3, 2).reshape(g * 512, n)

def pack4(w):
    words, scales = pack_weight(w, "e2m1")
    return words.reshape(words.shape[0], 128, -1), scales


def unpack4(words, scales):
    return unpack_weight(words.reshape(words.shape[0], 128, -1, 2), scales, "e2m1")


B, C, H, W, RQ, RV = 2, 1024, 64, 64, 4, 4
DQ, DV = C // RQ, C // RV
N = H * W


def maxpool2(x):
    b, c, h, w = x.shape
    return x.reshape(b, c, h // 2, 2, w // 2, 2).max(axis=(3, 5))


def setup_inputs():
    s = mx_kscale(C)
    imgs = bf(np.random.standard_normal((B, C, H, W)) * s[None, :, None, None])
    w_kv = np.random.standard_normal((DQ + DV, C)) * 0.5 / np.sqrt(C) / s[None, :]
    words, scales = pack4(np.ascontiguousarray(w_kv.T))
    return {"imgs": imgs, "w_kv_words": words, "w_kv_scales": scales}


def reference(imgs, w_kv_words, w_kv_scales):
    x = f64(imgs).reshape(B, C, N)
    kv = (unpack4(w_kv_words, w_kv_scales).T @ mxq(x, 1, "e4m3")).reshape(B, DQ + DV, H, W)
    return maxpool2(kv[:, :DQ]), maxpool2(kv[:, DQ:])

@@ -1,0 +1,152 @@
+from contextlib import ExitStack
+
+import concourse.mybir as mybir
+
+BF16 = mybir.dt.bfloat16
+F32 = mybir.dt.float32
+I32 = mybir.dt.int32
+U8 = mybir.dt.uint8
+U32 = mybir.dt.uint32
+FP8X4 = mybir.dt.float8_e4m3fn_x4
+FP4X4 = mybir.dt.float4_e2m1fn_x4
+
+P = 128
+PACK = 4
+IMAGES = 2
+CHANNELS = 1024
+SIDE = 64
+PIXELS = SIDE * SIDE
+OUT_ROWS = 512
+PASSES = CHANNELS // (P * PACK)
+ROW_TILES = OUT_ROWS // P
+ROW_TILES_PER_OUTPUT = ROW_TILES // 2
+
+CHUNK = 512
+CHUNKS_PER_IMAGE = PIXELS // CHUNK
+CHUNKS = IMAGES * CHUNKS_PER_IMAGE
+POOLED_CHUNK = CHUNK // 4
+POOLED_SIDE = SIDE // 2
+POOLED_PIXELS = PIXELS // 4
+
+LOAD_PIXELS = 1024
+CHUNKS_PER_LOAD = LOAD_PIXELS // CHUNK
+LOADS_PER_IMAGE = PIXELS // LOAD_PIXELS
+CHUNKS_PER_STORE = 2
+
+SCALAR_COLS = 448
+RUN = 4
+
+FLOPS = 2 * IMAGES * OUT_ROWS * CHANNELS * PIXELS
+
+
+def tile_selfattentionconv2d_pa_t_kernel(tc, imgs, w_kv_words, w_kv_scales, out_0, out_1):
+    nc = tc.nc
+    channel_rows = imgs.rearrange("b (g p t) h w -> b g p t (h w)", g=PASSES, p=P, t=PACK)
+    pooled_rows = [out.rearrange("b (r p) h w -> b p r (h w)", p=P) for out in (out_0, out_1)]
+
+    with ExitStack() as ctx:
+        consts = ctx.enter_context(tc.tile_pool(name="consts", bufs=1))
+        raw_pool = ctx.enter_context(tc.tile_pool(name="raw", bufs=IMAGES * LOADS_PER_IMAGE * PASSES))
+        grouped_pool = ctx.enter_context(tc.tile_pool(name="grouped", bufs=3))
+        quantised_pool = ctx.enter_context(tc.tile_pool(name="quantised", bufs=3))
+        pooled_pool = ctx.enter_context(tc.tile_pool(name="pooled", bufs=IMAGES))
+        psum = ctx.enter_context(tc.psum_pool(name="psum", bufs=2 * ROW_TILES))
+
+        raw = {}
+        grouped = {}
+        x_codes = {}
+        x_scales = {}
+        sums = {}
+        pooled = {}
+
+        def load_pixels(b, piece, g):
+            raw[(b, piece, g)] = raw_pool.tile([P, PACK, LOAD_PIXELS], BF16, name="raw")
+            nc.sync.dma_start(
+                out=raw[(b, piece, g)][:],
+                in_=channel_rows[b, g, :, :, piece * LOAD_PIXELS : (piece + 1) * LOAD_PIXELS],
+            )
+
+        def regroup(c):
+            b, in_image = divmod(c, CHUNKS_PER_IMAGE)
+            piece, in_piece = divmod(in_image, CHUNKS_PER_LOAD)
+            grouped[c] = grouped_pool.tile([P, PASSES, CHUNK, PACK], BF16, name="grouped", align_bytes=64)
+            for g in range(PASSES):
+                src = raw[(b, piece, g)][:, :, in_piece * CHUNK : (in_piece + 1) * CHUNK]
+                dst = grouped[c][:, g, :, :]
+                nc.scalar.copy(
+                    out=dst[:, :SCALAR_COLS, :].rearrange("p (n i) t -> p n t i", i=RUN),
+                    in_=src[:, :, :SCALAR_COLS].rearrange("p t (n i) -> p n t i", i=RUN),
+                )
+                nc.vector.tensor_copy(
+                    out=dst[:, SCALAR_COLS:, :].rearrange("p (n i) t -> p n t i", i=RUN),
+                    in_=src[:, :, SCALAR_COLS:].rearrange("p t (n i) -> p n t i", i=RUN),
+                )
+
+        def quantise(c):
+            x_codes[c] = quantised_pool.tile([P, PASSES, CHUNK], U32, name="x_codes", align_bytes=64)
+            x_scales[c] = quantised_pool.tile([P, PASSES, CHUNK], U8, name="x_scales", align_bytes=64)
+            nc.vector.quantize_mx(
+                out=x_codes[c][:].rearrange("p g n -> p (g n)").bitcast(FP8X4),
+                scales=x_scales[c][:].rearrange("p g n -> p (g n)"),
+                in_=grouped[c][:].rearrange("p g n t -> p (g n t)"),
+            )
+
+        def multiply(c):
+            for r in range(ROW_TILES):
+                sums[(c, r)] = psum.tile([P, CHUNK], F32, name="sums")
+                for g in range(PASSES):
+                    nc.tensor.matmul_mx(
+                        out=sums[(c, r)][:],
+                        lhsT=w_words[:, g, 2 * P * r : 2 * P * (r + 1)].bitcast(FP4X4),
+                        lhsT_scale=w_scales[:, g, P * r : P * (r + 1)],
+                        rhs=x_codes[c][:, g, :].bitcast(FP8X4),
+                        rhs_scale=x_scales[c][:, g, :],
+                        start=(g == 0),
+                        stop=(g == PASSES - 1),
+                    )
+
+        def pool_and_store(c):
+            b, in_image = divmod(c, CHUNKS_PER_IMAGE)
+            if in_image == 0:
+                pooled[b] = pooled_pool.tile([P, ROW_TILES, POOLED_PIXELS], F32, name="pooled")
+            for r in range(ROW_TILES):
+                nc.vector.tensor_reduce(
+                    out=pooled[b][:, r, in_image * POOLED_CHUNK : (in_image + 1) * POOLED_CHUNK].rearrange(
+                        "p (i j) -> p i j", j=POOLED_SIDE
+                    ),
+                    in_=sums[(c, r)][:].rearrange("p (i di j dj) -> p i j di dj", di=2, j=POOLED_SIDE, dj=2),
+                    axis=mybir.AxisListType.XY,
+                    op=mybir.AluOpType.max,
+                )
+            if (in_image + 1) % CHUNKS_PER_STORE == 0:
+                done = slice((in_image + 1 - CHUNKS_PER_STORE) * POOLED_CHUNK, (in_image + 1) * POOLED_CHUNK)
+                for which in range(2):
+                    first = which * ROW_TILES_PER_OUTPUT
+                    nc.sync.dma_start(
+                        out=pooled_rows[which][b, :, :, done],
+                        in_=pooled[b][:, first : first + ROW_TILES_PER_OUTPUT, done],
+                    )
+
+        w_words = consts.tile([P, PASSES, 2 * OUT_ROWS], U8, align_bytes=64)
+        nc.sync.dma_start(out=w_words[:].bitcast(I32), in_=w_kv_words.bitcast(I32).rearrange("g p n -> p g n"))
+        w_scales = consts.tile([P, PASSES, OUT_ROWS], U8, align_bytes=64)
+        nc.vector.memset(w_scales[:].bitcast(I32), 0)
+        for quadrant in range(4):
+            nc.sync.dma_start(
+                out=w_scales[32 * quadrant : 32 * quadrant + 4, :, :].bitcast(I32),
+                in_=w_kv_scales.bitcast(I32)[:, 4 * quadrant : 4 * quadrant + 4, :].rearrange("g q n -> q g n"),
+            )
+
+        for b in range(IMAGES):
+            for piece in range(LOADS_PER_IMAGE):
+                for g in range(PASSES):
+                    load_pixels(b, piece, g)
+
+        for step in range(CHUNKS + 2):
+            if step < CHUNKS:
+                regroup(step)
+            if 1 <= step <= CHUNKS:
+                quantise(step - 1)
+                multiply(step - 1)
+            if step >= 2:
+                pool_and_store(step - 2)

@@ -33,7 +33,7 @@ CHUNKS_PER_LOAD = LOAD_PIXELS // CHUNK
 LOADS_PER_IMAGE = PIXELS // LOAD_PIXELS
 CHUNKS_PER_STORE = 2
 
-SCALAR_COLS = 448
+GPSIMD_COLS = 256
 RUN = 4
 
 FLOPS = 2 * IMAGES * OUT_ROWS * CHANNELS * PIXELS
@@ -73,14 +73,19 @@ def tile_selfattentionconv2d_pa_t_kernel(tc, imgs, w_kv_words, w_kv_scales, out_
             for g in range(PASSES):
                 src = raw[(b, piece, g)][:, :, in_piece * CHUNK : (in_piece + 1) * CHUNK]
                 dst = grouped[c][:, g, :, :]
+                scalar_cols = CHUNK - GPSIMD_COLS if g == PASSES - 1 else CHUNK
                 nc.scalar.copy(
-                    out=dst[:, :SCALAR_COLS, :].rearrange("p (n i) t -> p n t i", i=RUN),
-                    in_=src[:, :, :SCALAR_COLS].rearrange("p t (n i) -> p n t i", i=RUN),
+                    out=dst[:, :scalar_cols, :].rearrange("p (n i) t -> p n t i", i=RUN),
+                    in_=src[:, :, :scalar_cols].rearrange("p t (n i) -> p n t i", i=RUN),
                 )
-                nc.vector.tensor_copy(
-                    out=dst[:, SCALAR_COLS:, :].rearrange("p (n i) t -> p n t i", i=RUN),
-                    in_=src[:, :, SCALAR_COLS:].rearrange("p t (n i) -> p n t i", i=RUN),
-                )
+            nc.gpsimd.tensor_scalar(
+                out=dst[:, CHUNK - GPSIMD_COLS :, :],
+                in0=src[:, :, CHUNK - GPSIMD_COLS :].rearrange("p t n -> p n t"),
+                scalar1=1.0,
+                scalar2=0.0,
+                op0=mybir.AluOpType.mult,
+                op1=mybir.AluOpType.add,
+            )
 
         def quantise(c):
             x_codes[c] = quantised_pool.tile([P, PASSES, CHUNK], U32, name="x_codes", align_bytes=64)

@@ -28,12 +28,11 @@ POOLED_CHUNK = CHUNK // 4
 POOLED_SIDE = SIDE // 2
 POOLED_PIXELS = PIXELS // 4
 
-LOAD_PIXELS = 1024
-CHUNKS_PER_LOAD = LOAD_PIXELS // CHUNK
-LOADS_PER_IMAGE = PIXELS // LOAD_PIXELS
+CHUNKS_PER_LOAD = 2
 CHUNKS_PER_STORE = 2
 
 GPSIMD_COLS = 256
+HEAD_CHUNKS = 1
 RUN = 4
 
 FLOPS = 2 * IMAGES * OUT_ROWS * CHANNELS * PIXELS
@@ -46,7 +45,7 @@ def tile_selfattentionconv2d_pa_t_kernel(tc, imgs, w_kv_words, w_kv_scales, out_
 
     with ExitStack() as ctx:
         consts = ctx.enter_context(tc.tile_pool(name="consts", bufs=1))
-        raw_pool = ctx.enter_context(tc.tile_pool(name="raw", bufs=IMAGES * LOADS_PER_IMAGE * PASSES))
+        raw_pool = ctx.enter_context(tc.tile_pool(name="raw", bufs=1))
         grouped_pool = ctx.enter_context(tc.tile_pool(name="grouped", bufs=3))
         quantised_pool = ctx.enter_context(tc.tile_pool(name="quantised", bufs=3))
         pooled_pool = ctx.enter_context(tc.tile_pool(name="pooled", bufs=IMAGES))
@@ -59,33 +58,43 @@ def tile_selfattentionconv2d_pa_t_kernel(tc, imgs, w_kv_words, w_kv_scales, out_
         sums = {}
         pooled = {}
 
-        def load_pixels(b, piece, g):
-            raw[(b, piece, g)] = raw_pool.tile([P, PACK, LOAD_PIXELS], BF16, name="raw")
-            nc.sync.dma_start(
-                out=raw[(b, piece, g)][:],
-                in_=channel_rows[b, g, :, :, piece * LOAD_PIXELS : (piece + 1) * LOAD_PIXELS],
+        def load_chunks(c, count):
+            b, in_image = divmod(c, CHUNKS_PER_IMAGE)
+            for g in range(PASSES):
+                landed = raw_pool.tile([P, PACK, count * CHUNK], BF16, name="raw_%d_%d" % (c, g))
+                nc.sync.dma_start(
+                    out=landed[:],
+                    in_=channel_rows[b, g, :, :, in_image * CHUNK : (in_image + count) * CHUNK],
+                )
+                for k in range(count):
+                    raw[(c + k, g)] = landed[:, :, k * CHUNK : (k + 1) * CHUNK]
+
+        def copy_in_runs(copy, dst, src):
+            copy(
+                out=dst.rearrange("p (n i) t -> p n t i", i=RUN),
+                in_=src.rearrange("p t (n i) -> p n t i", i=RUN),
             )
 
         def regroup(c):
-            b, in_image = divmod(c, CHUNKS_PER_IMAGE)
-            piece, in_piece = divmod(in_image, CHUNKS_PER_LOAD)
             grouped[c] = grouped_pool.tile([P, PASSES, CHUNK, PACK], BF16, name="grouped", align_bytes=64)
             for g in range(PASSES):
-                src = raw[(b, piece, g)][:, :, in_piece * CHUNK : (in_piece + 1) * CHUNK]
+                src = raw[(c, g)]
                 dst = grouped[c][:, g, :, :]
-                scalar_cols = CHUNK - GPSIMD_COLS if g == PASSES - 1 else CHUNK
-                nc.scalar.copy(
-                    out=dst[:, :scalar_cols, :].rearrange("p (n i) t -> p n t i", i=RUN),
-                    in_=src[:, :, :scalar_cols].rearrange("p t (n i) -> p n t i", i=RUN),
-                )
-            nc.gpsimd.tensor_scalar(
-                out=dst[:, CHUNK - GPSIMD_COLS :, :],
-                in0=src[:, :, CHUNK - GPSIMD_COLS :].rearrange("p t n -> p n t"),
-                scalar1=1.0,
-                scalar2=0.0,
-                op0=mybir.AluOpType.mult,
-                op1=mybir.AluOpType.add,
-            )
+                if c < HEAD_CHUNKS:
+                    copy_in_runs(nc.vector.tensor_copy, dst, src)
+                elif g < PASSES - 1:
+                    copy_in_runs(nc.scalar.copy, dst, src)
+                else:
+                    split = CHUNK - GPSIMD_COLS
+                    copy_in_runs(nc.scalar.copy, dst[:, :split, :], src[:, :, :split])
+                    nc.gpsimd.tensor_scalar(
+                        out=dst[:, split:, :],
+                        in0=src[:, :, split:].rearrange("p t n -> p n t"),
+                        scalar1=1.0,
+                        scalar2=0.0,
+                        op0=mybir.AluOpType.mult,
+                        op1=mybir.AluOpType.add,
+                    )
 
         def quantise(c):
             x_codes[c] = quantised_pool.tile([P, PASSES, CHUNK], U32, name="x_codes", align_bytes=64)
@@ -126,11 +135,12 @@ def tile_selfattentionconv2d_pa_t_kernel(tc, imgs, w_kv_words, w_kv_scales, out_
             if (in_image + 1) % CHUNKS_PER_STORE == 0:
                 done = slice((in_image + 1 - CHUNKS_PER_STORE) * POOLED_CHUNK, (in_image + 1) * POOLED_CHUNK)
                 for which in range(2):
-                    first = which * ROW_TILES_PER_OUTPUT
                     nc.sync.dma_start(
                         out=pooled_rows[which][b, :, :, done],
-                        in_=pooled[b][:, first : first + ROW_TILES_PER_OUTPUT, done],
+                        in_=pooled[b][:, which * ROW_TILES_PER_OUTPUT : (which + 1) * ROW_TILES_PER_OUTPUT, done],
                     )
+
+        load_chunks(0, 1)
 
         w_words = consts.tile([P, PASSES, 2 * OUT_ROWS], U8, align_bytes=64)
         nc.sync.dma_start(out=w_words[:].bitcast(I32), in_=w_kv_words.bitcast(I32).rearrange("g p n -> p g n"))
@@ -142,10 +152,9 @@ def tile_selfattentionconv2d_pa_t_kernel(tc, imgs, w_kv_words, w_kv_scales, out_
                 in_=w_kv_scales.bitcast(I32)[:, 4 * quadrant : 4 * quadrant + 4, :].rearrange("g q n -> q g n"),
             )
 
-        for b in range(IMAGES):
-            for piece in range(LOADS_PER_IMAGE):
-                for g in range(PASSES):
-                    load_pixels(b, piece, g)
+        load_chunks(1, CHUNKS_PER_LOAD - 1)
+        for c in range(CHUNKS_PER_LOAD, CHUNKS, CHUNKS_PER_LOAD):
+            load_chunks(c, CHUNKS_PER_LOAD)
 
         for step in range(CHUNKS + 2):
             if step < CHUNKS:

@@ -22,20 +22,19 @@ ROW_TILES = OUT_ROWS // P
 ROW_TILES_PER_OUTPUT = ROW_TILES // 2
 
 CHUNK = 512
+HALF = CHUNK // 2
 CHUNKS_PER_IMAGE = PIXELS // CHUNK
 CHUNKS = IMAGES * CHUNKS_PER_IMAGE
 POOLED_CHUNK = CHUNK // 4
 POOLED_SIDE = SIDE // 2
-POOLED_PIXELS = PIXELS // 4
-
-CHUNKS_PER_LOAD = 2
 CHUNKS_PER_STORE = 2
+STORES = CHUNKS // CHUNKS_PER_STORE
 
-GPSIMD_COLS = 256
-HEAD_CHUNKS = 1
 RUN = 4
 
 FLOPS = 2 * IMAGES * OUT_ROWS * CHANNELS * PIXELS
+
+assert PASSES == 2
 
 
 def tile_selfattentionconv2d_pa_t_kernel(tc, imgs, w_kv_words, w_kv_scales, out_0, out_1):
@@ -45,65 +44,78 @@ def tile_selfattentionconv2d_pa_t_kernel(tc, imgs, w_kv_words, w_kv_scales, out_
 
     with ExitStack() as ctx:
         consts = ctx.enter_context(tc.tile_pool(name="consts", bufs=1))
-        raw_pool = ctx.enter_context(tc.tile_pool(name="raw", bufs=1))
-        grouped_pool = ctx.enter_context(tc.tile_pool(name="grouped", bufs=3))
+        raw_pool = ctx.enter_context(tc.tile_pool(name="raw", bufs=CHUNKS * PASSES))
+        scalar_pool = ctx.enter_context(tc.tile_pool(name="by_scalar", bufs=3))
+        gpsimd_pool = ctx.enter_context(tc.tile_pool(name="by_gpsimd", bufs=1))
         quantised_pool = ctx.enter_context(tc.tile_pool(name="quantised", bufs=3))
-        pooled_pool = ctx.enter_context(tc.tile_pool(name="pooled", bufs=IMAGES))
+        pooled_pool = ctx.enter_context(tc.tile_pool(name="pooled", bufs=STORES))
         psum = ctx.enter_context(tc.psum_pool(name="psum", bufs=2 * ROW_TILES))
 
         raw = {}
-        grouped = {}
+        by_scalar = {}
+        by_gpsimd = {}
         x_codes = {}
         x_scales = {}
         sums = {}
         pooled = {}
 
-        def load_chunks(c, count):
+        def load(c):
             b, in_image = divmod(c, CHUNKS_PER_IMAGE)
             for g in range(PASSES):
-                landed = raw_pool.tile([P, PACK, count * CHUNK], BF16, name="raw_%d_%d" % (c, g))
+                raw[(c, g)] = raw_pool.tile([P, PACK, CHUNK], BF16, name="raw")
                 nc.sync.dma_start(
-                    out=landed[:],
-                    in_=channel_rows[b, g, :, :, in_image * CHUNK : (in_image + count) * CHUNK],
+                    out=raw[(c, g)][:],
+                    in_=channel_rows[b, g, :, :, in_image * CHUNK : (in_image + 1) * CHUNK],
                 )
-                for k in range(count):
-                    raw[(c + k, g)] = landed[:, :, k * CHUNK : (k + 1) * CHUNK]
 
-        def copy_in_runs(copy, dst, src):
-            copy(
-                out=dst.rearrange("p (n i) t -> p n t i", i=RUN),
-                in_=src.rearrange("p t (n i) -> p n t i", i=RUN),
+        def scalar_parts_of(c):
+            return (
+                (0, slice(0, CHUNK), by_scalar[c][:, :CHUNK, :]),
+                (1, slice(0, HALF), by_scalar[c][:, CHUNK:, :]),
             )
 
-        def regroup(c):
-            grouped[c] = grouped_pool.tile([P, PASSES, CHUNK, PACK], BF16, name="grouped", align_bytes=64)
-            for g in range(PASSES):
-                src = raw[(c, g)]
-                dst = grouped[c][:, g, :, :]
-                if c < HEAD_CHUNKS:
-                    copy_in_runs(nc.vector.tensor_copy, dst, src)
-                elif g < PASSES - 1:
-                    copy_in_runs(nc.scalar.copy, dst, src)
-                else:
-                    split = CHUNK - GPSIMD_COLS
-                    copy_in_runs(nc.scalar.copy, dst[:, :split, :], src[:, :, :split])
-                    nc.gpsimd.tensor_scalar(
-                        out=dst[:, split:, :],
-                        in0=src[:, :, split:].rearrange("p t n -> p n t"),
-                        scalar1=1.0,
-                        scalar2=0.0,
-                        op0=mybir.AluOpType.mult,
-                        op1=mybir.AluOpType.add,
-                    )
+        def gpsimd_part_of(c):
+            return (1, slice(HALF, CHUNK), by_gpsimd[c][:])
+
+        def copy_in_runs(copy, c, part):
+            g, cols, regrouped = part
+            copy(
+                out=regrouped.rearrange("p (n i) t -> p n t i", i=RUN),
+                in_=raw[(c, g)][:, :, cols].rearrange("p t (n i) -> p n t i", i=RUN),
+            )
+
+        def regroup_scalar_parts(c, copy=nc.scalar.copy):
+            by_scalar[c] = scalar_pool.tile([P, CHUNK + HALF, PACK], BF16, name="by_scalar", align_bytes=64)
+            for part in scalar_parts_of(c):
+                copy_in_runs(copy, c, part)
+
+        def copy_on_gpsimd(c, part):
+            g, cols, regrouped = part
+            nc.gpsimd.tensor_scalar(
+                out=regrouped,
+                in0=raw[(c, g)][:, :, cols].rearrange("p t n -> p n t"),
+                scalar1=1.0,
+                scalar2=0.0,
+                op0=mybir.AluOpType.mult,
+                op1=mybir.AluOpType.add,
+            )
+
+        def regroup_gpsimd_part(c, by_vector=False):
+            by_gpsimd[c] = gpsimd_pool.tile([P, HALF, PACK], BF16, name="by_gpsimd", align_bytes=64)
+            if by_vector:
+                copy_in_runs(nc.vector.tensor_copy, c, gpsimd_part_of(c))
+            else:
+                copy_on_gpsimd(c, gpsimd_part_of(c))
 
         def quantise(c):
             x_codes[c] = quantised_pool.tile([P, PASSES, CHUNK], U32, name="x_codes", align_bytes=64)
             x_scales[c] = quantised_pool.tile([P, PASSES, CHUNK], U8, name="x_scales", align_bytes=64)
-            nc.vector.quantize_mx(
-                out=x_codes[c][:].rearrange("p g n -> p (g n)").bitcast(FP8X4),
-                scales=x_scales[c][:].rearrange("p g n -> p (g n)"),
-                in_=grouped[c][:].rearrange("p g n t -> p (g n t)"),
-            )
+            for g, cols, regrouped in scalar_parts_of(c) + (gpsimd_part_of(c),):
+                nc.vector.quantize_mx(
+                    out=x_codes[c][:, g, cols].bitcast(FP8X4),
+                    scales=x_scales[c][:, g, cols],
+                    in_=regrouped.rearrange("p n t -> p (n t)"),
+                )
 
         def multiply(c):
             for r in range(ROW_TILES):
@@ -119,28 +131,32 @@ def tile_selfattentionconv2d_pa_t_kernel(tc, imgs, w_kv_words, w_kv_scales, out_
                         stop=(g == PASSES - 1),
                     )
 
-        def pool_and_store(c):
-            b, in_image = divmod(c, CHUNKS_PER_IMAGE)
-            if in_image == 0:
-                pooled[b] = pooled_pool.tile([P, ROW_TILES, POOLED_PIXELS], F32, name="pooled")
-            for r in range(ROW_TILES):
+        def pool(c, row_tiles):
+            store, in_store = divmod(c, CHUNKS_PER_STORE)
+            if store not in pooled:
+                pooled[store] = pooled_pool.tile(
+                    [P, ROW_TILES, CHUNKS_PER_STORE * POOLED_CHUNK], F32, name="pooled"
+                )
+            for r in row_tiles:
                 nc.vector.tensor_reduce(
-                    out=pooled[b][:, r, in_image * POOLED_CHUNK : (in_image + 1) * POOLED_CHUNK].rearrange(
+                    out=pooled[store][:, r, in_store * POOLED_CHUNK : (in_store + 1) * POOLED_CHUNK].rearrange(
                         "p (i j) -> p i j", j=POOLED_SIDE
                     ),
                     in_=sums[(c, r)][:].rearrange("p (i di j dj) -> p i j di dj", di=2, j=POOLED_SIDE, dj=2),
                     axis=mybir.AxisListType.XY,
                     op=mybir.AluOpType.max,
                 )
-            if (in_image + 1) % CHUNKS_PER_STORE == 0:
-                done = slice((in_image + 1 - CHUNKS_PER_STORE) * POOLED_CHUNK, (in_image + 1) * POOLED_CHUNK)
-                for which in range(2):
-                    nc.sync.dma_start(
-                        out=pooled_rows[which][b, :, :, done],
-                        in_=pooled[b][:, which * ROW_TILES_PER_OUTPUT : (which + 1) * ROW_TILES_PER_OUTPUT, done],
-                    )
 
-        load_chunks(0, 1)
+        def store_pooled(store):
+            b, in_image = divmod(store * CHUNKS_PER_STORE, CHUNKS_PER_IMAGE)
+            done = slice(in_image * POOLED_CHUNK, (in_image + CHUNKS_PER_STORE) * POOLED_CHUNK)
+            for which in range(2):
+                nc.sync.dma_start(
+                    out=pooled_rows[which][b, :, :, done],
+                    in_=pooled[store][:, which * ROW_TILES_PER_OUTPUT : (which + 1) * ROW_TILES_PER_OUTPUT, :],
+                )
+
+        load(0)
 
         w_words = consts.tile([P, PASSES, 2 * OUT_ROWS], U8, align_bytes=64)
         nc.sync.dma_start(out=w_words[:].bitcast(I32), in_=w_kv_words.bitcast(I32).rearrange("g p n -> p g n"))
@@ -152,15 +168,25 @@ def tile_selfattentionconv2d_pa_t_kernel(tc, imgs, w_kv_words, w_kv_scales, out_
                 in_=w_kv_scales.bitcast(I32)[:, 4 * quadrant : 4 * quadrant + 4, :].rearrange("g q n -> q g n"),
             )
 
-        load_chunks(1, CHUNKS_PER_LOAD - 1)
-        for c in range(CHUNKS_PER_LOAD, CHUNKS, CHUNKS_PER_LOAD):
-            load_chunks(c, CHUNKS_PER_LOAD)
+        for c in range(1, CHUNKS):
+            load(c)
 
-        for step in range(CHUNKS + 2):
-            if step < CHUNKS:
-                regroup(step)
-            if 1 <= step <= CHUNKS:
-                quantise(step - 1)
-                multiply(step - 1)
-            if step >= 2:
-                pool_and_store(step - 2)
+        with tc.manual_schedule():
+            regroup_scalar_parts(0, copy=nc.vector.tensor_copy)
+            regroup_gpsimd_part(0, by_vector=True)
+            quantise(0)
+            multiply(0)
+            regroup_scalar_parts(1)
+            regroup_gpsimd_part(1)
+            for c in range(CHUNKS):
+                if c + 2 < CHUNKS:
+                    regroup_scalar_parts(c + 2)
+                pool(c, range(0, ROW_TILES // 2))
+                if c + 1 < CHUNKS:
+                    quantise(c + 1)
+                    multiply(c + 1)
+                if c + 2 < CHUNKS:
+                    regroup_gpsimd_part(c + 2)
+                pool(c, range(ROW_TILES // 2, ROW_TILES))
+                if (c + 1) % CHUNKS_PER_STORE == 0:
+                    store_pooled(c // CHUNKS_PER_STORE)

@@ -1,6 +1,7 @@
 from contextlib import ExitStack
 
 import concourse.mybir as mybir
+from concourse.masks import make_identity
 
 BF16 = mybir.dt.bfloat16
 F32 = mybir.dt.float32
@@ -30,6 +31,10 @@ POOLED_SIDE = SIDE // 2
 CHUNKS_PER_STORE = 2
 STORES = CHUNKS // CHUNKS_PER_STORE
 
+BANK_PIXELS = 256
+MOVING_PIXELS = 128
+WARM_UP = 6
+
 RUN = 4
 
 FLOPS = 2 * IMAGES * OUT_ROWS * CHANNELS * PIXELS
@@ -44,11 +49,11 @@ def tile_selfattentionconv2d_pa_t_kernel(tc, imgs, w_kv_words, w_kv_scales, out_
 
     with ExitStack() as ctx:
         consts = ctx.enter_context(tc.tile_pool(name="consts", bufs=1))
-        raw_pool = ctx.enter_context(tc.tile_pool(name="raw", bufs=CHUNKS * PASSES))
+        raw_pool = ctx.enter_context(tc.tile_pool(name="raw", bufs=CHUNKS * PASSES + 2))
         scalar_pool = ctx.enter_context(tc.tile_pool(name="by_scalar", bufs=3))
         gpsimd_pool = ctx.enter_context(tc.tile_pool(name="by_gpsimd", bufs=1))
         quantised_pool = ctx.enter_context(tc.tile_pool(name="quantised", bufs=3))
-        pooled_pool = ctx.enter_context(tc.tile_pool(name="pooled", bufs=STORES))
+        pooled_pool = ctx.enter_context(tc.tile_pool(name="pooled", bufs=2 * (STORES + 1)))
         psum = ctx.enter_context(tc.psum_pool(name="psum", bufs=2 * ROW_TILES))
 
         raw = {}
@@ -61,12 +66,22 @@ def tile_selfattentionconv2d_pa_t_kernel(tc, imgs, w_kv_words, w_kv_scales, out_
 
         def load(c):
             b, in_image = divmod(c, CHUNKS_PER_IMAGE)
+            width = load_width(c)
             for g in range(PASSES):
-                raw[(c, g)] = raw_pool.tile([P, PACK, CHUNK], BF16, name="raw")
-                nc.sync.dma_start(
-                    out=raw[(c, g)][:],
-                    in_=channel_rows[b, g, :, :, in_image * CHUNK : (in_image + 1) * CHUNK],
-                )
+                for first in range(0, CHUNK, width):
+                    raw[(c, g, first)] = raw_pool.tile([P, PACK, width], BF16, name="raw")
+                    nc.sync.dma_start(
+                        out=raw[(c, g, first)][:],
+                        in_=channel_rows[b, g, :, :, in_image * CHUNK + first : in_image * CHUNK + first + width],
+                    )
+
+        def load_width(c):
+            return HALF if c == 0 else CHUNK
+
+        def raw_pixels(c, g, cols):
+            first = cols.start - cols.start % load_width(c)
+            assert cols.stop <= first + load_width(c)
+            return raw[(c, g, first)][:, :, cols.start - first : cols.stop - first]
 
         def scalar_parts_of(c):
             return (
@@ -81,80 +96,125 @@ def tile_selfattentionconv2d_pa_t_kernel(tc, imgs, w_kv_words, w_kv_scales, out_
             g, cols, regrouped = part
             copy(
                 out=regrouped.rearrange("p (n i) t -> p n t i", i=RUN),
-                in_=raw[(c, g)][:, :, cols].rearrange("p t (n i) -> p n t i", i=RUN),
+                in_=raw_pixels(c, g, cols).rearrange("p t (n i) -> p n t i", i=RUN),
             )
 
-        def regroup_scalar_parts(c, copy=nc.scalar.copy):
+        def regroup_scalar_parts(c):
             by_scalar[c] = scalar_pool.tile([P, CHUNK + HALF, PACK], BF16, name="by_scalar", align_bytes=64)
-            for part in scalar_parts_of(c):
-                copy_in_runs(copy, c, part)
+            whole_pass, half_pass = scalar_parts_of(c)
+            copy_in_runs(nc.scalar.copy, c, whole_pass)
+            regroup_through_tensor(c, half_pass, nc.scalar.copy)
+
+        def regroup_first_chunk(g):
+            if g == 0:
+                by_scalar[0] = scalar_pool.tile([P, CHUNK + HALF, PACK], BF16, name="by_scalar", align_bytes=64)
+                by_gpsimd[0] = gpsimd_pool.tile([P, HALF, PACK], BF16, name="by_gpsimd", align_bytes=64)
+                copy_in_runs(nc.scalar.copy, 0, gpsimd_part_of(0))
+                copy_in_runs(nc.vector.tensor_copy, 0, (0, slice(0, HALF), by_scalar[0][:, :HALF, :]))
+                copy_in_runs(nc.vector.tensor_copy, 0, (0, slice(HALF, CHUNK), by_scalar[0][:, HALF:CHUNK, :]))
+            else:
+                copy_in_runs(nc.vector.tensor_copy, 0, (1, slice(0, HALF), by_scalar[0][:, CHUNK:, :]))
+
+        def regroup_through_tensor(c, part, copy):
+            g, cols, regrouped = part
+            assert cols.stop - cols.start == BANK_PIXELS
+            bank = psum.tile([P, BANK_PIXELS * PACK], BF16, name="sums")
+            for at in range(0, BANK_PIXELS, MOVING_PIXELS):
+                nc.tensor.matmul(
+                    out=bank[:, at * PACK : (at + MOVING_PIXELS) * PACK].rearrange("p (n t) -> p n t", t=PACK),
+                    lhsT=identity[:],
+                    rhs=raw_pixels(c, g, slice(cols.start + at, cols.start + at + MOVING_PIXELS)).rearrange(
+                        "p t n -> p n t"
+                    ),
+                    start=True,
+                    stop=True,
+                )
+            copy(out=regrouped.rearrange("p n t -> p (n t)"), in_=bank[:])
 
         def copy_on_gpsimd(c, part):
             g, cols, regrouped = part
             nc.gpsimd.tensor_scalar(
                 out=regrouped,
-                in0=raw[(c, g)][:, :, cols].rearrange("p t n -> p n t"),
+                in0=raw_pixels(c, g, cols).rearrange("p t n -> p n t"),
                 scalar1=1.0,
                 scalar2=0.0,
                 op0=mybir.AluOpType.mult,
                 op1=mybir.AluOpType.add,
             )
 
-        def regroup_gpsimd_part(c, by_vector=False):
+        def regroup_gpsimd_part(c):
             by_gpsimd[c] = gpsimd_pool.tile([P, HALF, PACK], BF16, name="by_gpsimd", align_bytes=64)
-            if by_vector:
-                copy_in_runs(nc.vector.tensor_copy, c, gpsimd_part_of(c))
-            else:
-                copy_on_gpsimd(c, gpsimd_part_of(c))
+            copy_on_gpsimd(c, gpsimd_part_of(c))
 
-        def quantise(c):
-            x_codes[c] = quantised_pool.tile([P, PASSES, CHUNK], U32, name="x_codes", align_bytes=64)
-            x_scales[c] = quantised_pool.tile([P, PASSES, CHUNK], U8, name="x_scales", align_bytes=64)
+        def quantise(c, passes=(0, 1)):
+            if c not in x_codes:
+                x_codes[c] = quantised_pool.tile([P, PASSES, CHUNK], U32, name="x_codes", align_bytes=64)
+                x_scales[c] = quantised_pool.tile([P, PASSES, CHUNK], U8, name="x_scales", align_bytes=64)
             for g, cols, regrouped in scalar_parts_of(c) + (gpsimd_part_of(c),):
-                nc.vector.quantize_mx(
-                    out=x_codes[c][:, g, cols].bitcast(FP8X4),
-                    scales=x_scales[c][:, g, cols],
-                    in_=regrouped.rearrange("p n t -> p (n t)"),
-                )
+                if g in passes:
+                    nc.vector.quantize_mx(
+                        out=x_codes[c][:, g, cols].bitcast(FP8X4),
+                        scales=x_scales[c][:, g, cols],
+                        in_=regrouped.rearrange("p n t -> p (n t)"),
+                    )
+
+        def one_pass(c, r, g):
+            if g == 0:
+                sums[(c, r)] = psum.tile([P, CHUNK], F32, name="sums")
+            nc.tensor.matmul_mx(
+                out=sums[(c, r)][:],
+                lhsT=w_words[:, g, 2 * P * r : 2 * P * (r + 1)].bitcast(FP4X4),
+                lhsT_scale=w_scales[:, g, P * r : P * (r + 1)],
+                rhs=x_codes[c][:, g, :].bitcast(FP8X4),
+                rhs_scale=x_scales[c][:, g, :],
+                start=(g == 0),
+                stop=(g == PASSES - 1),
+            )
 
         def multiply(c):
             for r in range(ROW_TILES):
-                sums[(c, r)] = psum.tile([P, CHUNK], F32, name="sums")
                 for g in range(PASSES):
-                    nc.tensor.matmul_mx(
-                        out=sums[(c, r)][:],
-                        lhsT=w_words[:, g, 2 * P * r : 2 * P * (r + 1)].bitcast(FP4X4),
-                        lhsT_scale=w_scales[:, g, P * r : P * (r + 1)],
-                        rhs=x_codes[c][:, g, :].bitcast(FP8X4),
-                        rhs_scale=x_scales[c][:, g, :],
-                        start=(g == 0),
-                        stop=(g == PASSES - 1),
-                    )
+                    one_pass(c, r, g)
+
+        def warm_up():
+            unread = psum.tile([P, CHUNK], F32, name="sums")
+            for i in range(WARM_UP):
+                nc.tensor.matmul(out=unread[:], lhsT=zeros[:, :P], rhs=zeros[:], start=True, stop=True)
+
+        def store_of(c):
+            if c >= CHUNKS - CHUNKS_PER_STORE:
+                return c, 1
+            return c - c % CHUNKS_PER_STORE, CHUNKS_PER_STORE
 
         def pool(c, row_tiles):
-            store, in_store = divmod(c, CHUNKS_PER_STORE)
-            if store not in pooled:
-                pooled[store] = pooled_pool.tile(
-                    [P, ROW_TILES, CHUNKS_PER_STORE * POOLED_CHUNK], F32, name="pooled"
-                )
+            first, chunks = store_of(c)
             for r in row_tiles:
+                which, row_tile = divmod(r, ROW_TILES_PER_OUTPUT)
+                if (first, which) not in pooled:
+                    pooled[(first, which)] = pooled_pool.tile(
+                        [P, ROW_TILES_PER_OUTPUT, chunks * POOLED_CHUNK], F32, name="pooled"
+                    )
                 nc.vector.tensor_reduce(
-                    out=pooled[store][:, r, in_store * POOLED_CHUNK : (in_store + 1) * POOLED_CHUNK].rearrange(
-                        "p (i j) -> p i j", j=POOLED_SIDE
-                    ),
+                    out=pooled[(first, which)][
+                        :, row_tile, (c - first) * POOLED_CHUNK : (c - first + 1) * POOLED_CHUNK
+                    ].rearrange("p (i j) -> p i j", j=POOLED_SIDE),
                     in_=sums[(c, r)][:].rearrange("p (i di j dj) -> p i j di dj", di=2, j=POOLED_SIDE, dj=2),
                     axis=mybir.AxisListType.XY,
                     op=mybir.AluOpType.max,
                 )
+                if c == first + chunks - 1 and row_tile == ROW_TILES_PER_OUTPUT - 1:
+                    b, in_image = divmod(first, CHUNKS_PER_IMAGE)
+                    nc.sync.dma_start(
+                        out=pooled_rows[which][
+                            b, :, :, in_image * POOLED_CHUNK : (in_image + chunks) * POOLED_CHUNK
+                        ],
+                        in_=pooled[(first, which)][:],
+                    )
 
-        def store_pooled(store):
-            b, in_image = divmod(store * CHUNKS_PER_STORE, CHUNKS_PER_IMAGE)
-            done = slice(in_image * POOLED_CHUNK, (in_image + CHUNKS_PER_STORE) * POOLED_CHUNK)
-            for which in range(2):
-                nc.sync.dma_start(
-                    out=pooled_rows[which][b, :, :, done],
-                    in_=pooled[store][:, which * ROW_TILES_PER_OUTPUT : (which + 1) * ROW_TILES_PER_OUTPUT, :],
-                )
+        zeros = consts.tile([P, CHUNK], BF16)
+        nc.vector.memset(zeros[:], 0.0)
+        identity = consts.tile([P, P], BF16)
+        make_identity(nc, identity[:])
 
         load(0)
 
@@ -172,21 +232,22 @@ def tile_selfattentionconv2d_pa_t_kernel(tc, imgs, w_kv_words, w_kv_scales, out_
             load(c)
 
         with tc.manual_schedule():
-            regroup_scalar_parts(0, copy=nc.vector.tensor_copy)
-            regroup_gpsimd_part(0, by_vector=True)
-            quantise(0)
-            multiply(0)
+            warm_up()
+            for g in range(PASSES):
+                regroup_first_chunk(g)
+                quantise(0, passes=(g,))
+                for r in range(ROW_TILES):
+                    one_pass(0, r, g)
             regroup_scalar_parts(1)
             regroup_gpsimd_part(1)
             for c in range(CHUNKS):
                 if c + 2 < CHUNKS:
                     regroup_scalar_parts(c + 2)
-                pool(c, range(0, ROW_TILES // 2))
+                before = ROW_TILES if c == 0 else ROW_TILES // 2
+                pool(c, range(0, before))
                 if c + 1 < CHUNKS:
                     quantise(c + 1)
                     multiply(c + 1)
                 if c + 2 < CHUNKS:
                     regroup_gpsimd_part(c + 2)
-                pool(c, range(ROW_TILES // 2, ROW_TILES))
-                if (c + 1) % CHUNKS_PER_STORE == 0:
-                    store_pooled(c // CHUNKS_PER_STORE)
+                pool(c, range(before, ROW_TILES))

@@ -24,6 +24,7 @@ ROW_TILES_PER_OUTPUT = ROW_TILES // 2
 
 CHUNK = 512
 HALF = CHUNK // 2
+GPSIMD_PIXELS = 256
 CHUNKS_PER_IMAGE = PIXELS // CHUNK
 CHUNKS = IMAGES * CHUNKS_PER_IMAGE
 POOLED_CHUNK = CHUNK // 4
@@ -49,7 +50,7 @@ def tile_selfattentionconv2d_pa_t_kernel(tc, imgs, w_kv_words, w_kv_scales, out_
 
     with ExitStack() as ctx:
         consts = ctx.enter_context(tc.tile_pool(name="consts", bufs=1))
-        raw_pool = ctx.enter_context(tc.tile_pool(name="raw", bufs=CHUNKS * PASSES + 2))
+        raw_pool = ctx.enter_context(tc.tile_pool(name="raw", bufs=CHUNKS * PASSES + 1))
         scalar_pool = ctx.enter_context(tc.tile_pool(name="by_scalar", bufs=3))
         gpsimd_pool = ctx.enter_context(tc.tile_pool(name="by_gpsimd", bufs=1))
         quantised_pool = ctx.enter_context(tc.tile_pool(name="quantised", bufs=3))
@@ -66,8 +67,8 @@ def tile_selfattentionconv2d_pa_t_kernel(tc, imgs, w_kv_words, w_kv_scales, out_
 
         def load(c):
             b, in_image = divmod(c, CHUNKS_PER_IMAGE)
-            width = load_width(c)
             for g in range(PASSES):
+                width = load_width(c, g)
                 for first in range(0, CHUNK, width):
                     raw[(c, g, first)] = raw_pool.tile([P, PACK, width], BF16, name="raw")
                     nc.sync.dma_start(
@@ -75,22 +76,36 @@ def tile_selfattentionconv2d_pa_t_kernel(tc, imgs, w_kv_words, w_kv_scales, out_
                         in_=channel_rows[b, g, :, :, in_image * CHUNK + first : in_image * CHUNK + first + width],
                     )
 
-        def load_width(c):
-            return HALF if c == 0 else CHUNK
+        def load_width(c, g):
+            return HALF if (c, g) == (0, 0) else CHUNK
 
         def raw_pixels(c, g, cols):
-            first = cols.start - cols.start % load_width(c)
-            assert cols.stop <= first + load_width(c)
+            first = cols.start - cols.start % load_width(c, g)
+            assert cols.stop <= first + load_width(c, g)
             return raw[(c, g, first)][:, :, cols.start - first : cols.stop - first]
 
         def scalar_parts_of(c):
             return (
                 (0, slice(0, CHUNK), by_scalar[c][:, :CHUNK, :]),
-                (1, slice(0, HALF), by_scalar[c][:, CHUNK:, :]),
+                (1, slice(0, CHUNK - last_pixels(c)), by_scalar[c][:, CHUNK:, :]),
             )
 
+        def last_pixels(c):
+            return HALF if c == 0 else GPSIMD_PIXELS
+
+        def in_allowed_widths(part):
+            g, cols, regrouped = part
+            pieces = []
+            at = cols.start
+            for width in (512, 256, 128, 64):
+                if cols.stop - at >= width:
+                    pieces.append((g, slice(at, at + width), regrouped[:, at - cols.start : at - cols.start + width, :]))
+                    at += width
+            assert at == cols.stop
+            return pieces
+
         def gpsimd_part_of(c):
-            return (1, slice(HALF, CHUNK), by_gpsimd[c][:])
+            return (1, slice(CHUNK - last_pixels(c), CHUNK), by_gpsimd[c][:])
 
         def copy_in_runs(copy, c, part):
             g, cols, regrouped = part
@@ -100,10 +115,11 @@ def tile_selfattentionconv2d_pa_t_kernel(tc, imgs, w_kv_words, w_kv_scales, out_
             )
 
         def regroup_scalar_parts(c):
-            by_scalar[c] = scalar_pool.tile([P, CHUNK + HALF, PACK], BF16, name="by_scalar", align_bytes=64)
-            whole_pass, half_pass = scalar_parts_of(c)
-            copy_in_runs(nc.scalar.copy, c, whole_pass)
-            regroup_through_tensor(c, half_pass, nc.scalar.copy)
+            by_scalar[c] = scalar_pool.tile(
+                [P, 2 * CHUNK - GPSIMD_PIXELS, PACK], BF16, name="by_scalar", align_bytes=64
+            )
+            for part in scalar_parts_of(c):
+                copy_in_runs(nc.scalar.copy, c, part)
 
         def regroup_first_chunk(g):
             if g == 0:
@@ -143,14 +159,17 @@ def tile_selfattentionconv2d_pa_t_kernel(tc, imgs, w_kv_words, w_kv_scales, out_
             )
 
         def regroup_gpsimd_part(c):
-            by_gpsimd[c] = gpsimd_pool.tile([P, HALF, PACK], BF16, name="by_gpsimd", align_bytes=64)
+            by_gpsimd[c] = gpsimd_pool.tile([P, GPSIMD_PIXELS, PACK], BF16, name="by_gpsimd", align_bytes=64)
             copy_on_gpsimd(c, gpsimd_part_of(c))
 
         def quantise(c, passes=(0, 1)):
             if c not in x_codes:
                 x_codes[c] = quantised_pool.tile([P, PASSES, CHUNK], U32, name="x_codes", align_bytes=64)
                 x_scales[c] = quantised_pool.tile([P, PASSES, CHUNK], U8, name="x_scales", align_bytes=64)
-            for g, cols, regrouped in scalar_parts_of(c) + (gpsimd_part_of(c),):
+            pieces = []
+            for part in scalar_parts_of(c) + (gpsimd_part_of(c),):
+                pieces.extend(in_allowed_widths(part))
+            for g, cols, regrouped in pieces:
                 if g in passes:
                     nc.vector.quantize_mx(
                         out=x_codes[c][:, g, cols].bitcast(FP8X4),
@@ -243,7 +262,7 @@ def tile_selfattentionconv2d_pa_t_kernel(tc, imgs, w_kv_words, w_kv_scales, out_
             for c in range(CHUNKS):
                 if c + 2 < CHUNKS:
                     regroup_scalar_parts(c + 2)
-                before = ROW_TILES if c == 0 else ROW_TILES // 2
+                before = ROW_TILES // 2
                 pool(c, range(0, before))
                 if c + 1 < CHUNKS:
                     quantise(c + 1)

@@ -36,7 +36,7 @@ BANK_PIXELS = 256
 MOVING_PIXELS = 128
 WARM_UP = 6
 
-RUN = 4
+RUN = 8
 
 FLOPS = 2 * IMAGES * OUT_ROWS * CHANNELS * PIXELS
 

@@ -118,8 +118,13 @@ def tile_selfattentionconv2d_pa_t_kernel(tc, imgs, w_kv_words, w_kv_scales, out_
             by_scalar[c] = scalar_pool.tile(
                 [P, 2 * CHUNK - GPSIMD_PIXELS, PACK], BF16, name="by_scalar", align_bytes=64
             )
-            for part in scalar_parts_of(c):
-                copy_in_runs(nc.scalar.copy, c, part)
+            whole_pass, rest = scalar_parts_of(c)
+            if c == 1:
+                copy_in_runs(nc.vector.tensor_copy, c, (0, slice(0, HALF), by_scalar[c][:, :HALF, :]))
+                copy_in_runs(nc.scalar.copy, c, (0, slice(HALF, CHUNK), by_scalar[c][:, HALF:CHUNK, :]))
+            else:
+                copy_in_runs(nc.scalar.copy, c, whole_pass)
+            copy_in_runs(nc.scalar.copy, c, rest)
 
         def regroup_first_chunk(g):
             if g == 0:

@@ -32,8 +32,7 @@ POOLED_SIDE = SIDE // 2
 CHUNKS_PER_STORE = 2
 STORES = CHUNKS // CHUNKS_PER_STORE
 
-BANK_PIXELS = 256
-MOVING_PIXELS = 128
+FIRST_ON_TENSOR = 3
 WARM_UP = 6
 
 RUN = 8
@@ -55,11 +54,13 @@ def tile_selfattentionconv2d_pa_t_kernel(tc, imgs, w_kv_words, w_kv_scales, out_
         gpsimd_pool = ctx.enter_context(tc.tile_pool(name="by_gpsimd", bufs=1))
         quantised_pool = ctx.enter_context(tc.tile_pool(name="quantised", bufs=3))
         pooled_pool = ctx.enter_context(tc.tile_pool(name="pooled", bufs=2 * (STORES + 1)))
-        psum = ctx.enter_context(tc.psum_pool(name="psum", bufs=2 * ROW_TILES))
+        psum = ctx.enter_context(tc.psum_pool(name="psum", bufs=ROW_TILES + ROW_TILES // 2))
+        regroup_psum = ctx.enter_context(tc.psum_pool(name="regroup_psum", bufs=2))
 
         raw = {}
         by_scalar = {}
         by_gpsimd = {}
+        through_tensor = {}
         x_codes = {}
         x_scales = {}
         sums = {}
@@ -124,7 +125,10 @@ def tile_selfattentionconv2d_pa_t_kernel(tc, imgs, w_kv_words, w_kv_scales, out_
                 copy_in_runs(nc.scalar.copy, c, (0, slice(HALF, CHUNK), by_scalar[c][:, HALF:CHUNK, :]))
             else:
                 copy_in_runs(nc.scalar.copy, c, whole_pass)
-            copy_in_runs(nc.scalar.copy, c, rest)
+            if c in through_tensor:
+                nc.scalar.copy(out=rest[2].rearrange("p n t -> p (n t)"), in_=through_tensor[c][:])
+            else:
+                copy_in_runs(nc.scalar.copy, c, rest)
 
         def regroup_first_chunk(g):
             if g == 0:
@@ -136,21 +140,17 @@ def tile_selfattentionconv2d_pa_t_kernel(tc, imgs, w_kv_words, w_kv_scales, out_
             else:
                 copy_in_runs(nc.vector.tensor_copy, 0, (1, slice(0, HALF), by_scalar[0][:, CHUNK:, :]))
 
-        def regroup_through_tensor(c, part, copy):
-            g, cols, regrouped = part
-            assert cols.stop - cols.start == BANK_PIXELS
-            bank = psum.tile([P, BANK_PIXELS * PACK], BF16, name="sums")
-            for at in range(0, BANK_PIXELS, MOVING_PIXELS):
+        def regroup_on_tensor(c):
+            through_tensor[c] = regroup_psum.tile([P, HALF * PACK], BF16, name="regrouped_in_psum")
+            pixels = raw_pixels(c, 1, slice(0, HALF))
+            for t in range(0, PACK, 2):
                 nc.tensor.matmul(
-                    out=bank[:, at * PACK : (at + MOVING_PIXELS) * PACK].rearrange("p (n t) -> p n t", t=PACK),
+                    out=through_tensor[c][:].rearrange("p (n t) -> p t n", t=PACK)[:, t : t + 2, :],
                     lhsT=identity[:],
-                    rhs=raw_pixels(c, g, slice(cols.start + at, cols.start + at + MOVING_PIXELS)).rearrange(
-                        "p t n -> p n t"
-                    ),
+                    rhs=pixels[:, t : t + 2, :],
                     start=True,
                     stop=True,
                 )
-            copy(out=regrouped.rearrange("p n t -> p (n t)"), in_=bank[:])
 
         def copy_on_gpsimd(c, part):
             g, cols, regrouped = part
@@ -272,6 +272,8 @@ def tile_selfattentionconv2d_pa_t_kernel(tc, imgs, w_kv_words, w_kv_scales, out_
                 if c + 1 < CHUNKS:
                     quantise(c + 1)
                     multiply(c + 1)
+                if FIRST_ON_TENSOR <= c + 3 < CHUNKS:
+                    regroup_on_tensor(c + 3)
                 if c + 2 < CHUNKS:
                     regroup_gpsimd_part(c + 2)
                 pool(c, range(before, ROW_TILES))

@@ -33,6 +33,7 @@ CHUNKS_PER_STORE = 2
 STORES = CHUNKS // CHUNKS_PER_STORE
 
 FIRST_ON_TENSOR = 3
+HELPED = range(3, 15)
 WARM_UP = 6
 
 RUN = 8
@@ -54,6 +55,8 @@ def tile_selfattentionconv2d_pa_t_kernel(tc, imgs, w_kv_words, w_kv_scales, out_
         gpsimd_pool = ctx.enter_context(tc.tile_pool(name="by_gpsimd", bufs=1))
         quantised_pool = ctx.enter_context(tc.tile_pool(name="quantised", bufs=3))
         pooled_pool = ctx.enter_context(tc.tile_pool(name="pooled", bufs=2 * (STORES + 1)))
+        left_pool = ctx.enter_context(tc.tile_pool(name="left", bufs=2))
+        row_max_pool = ctx.enter_context(tc.tile_pool(name="row_max", bufs=2))
         psum = ctx.enter_context(tc.psum_pool(name="psum", bufs=ROW_TILES + ROW_TILES // 2))
         regroup_psum = ctx.enter_context(tc.psum_pool(name="regroup_psum", bufs=2))
 
@@ -64,6 +67,8 @@ def tile_selfattentionconv2d_pa_t_kernel(tc, imgs, w_kv_words, w_kv_scales, out_
         x_codes = {}
         x_scales = {}
         sums = {}
+        left = {}
+        row_max = {}
         pooled = {}
 
         def load(c):
@@ -115,16 +120,19 @@ def tile_selfattentionconv2d_pa_t_kernel(tc, imgs, w_kv_words, w_kv_scales, out_
                 in_=raw_pixels(c, g, cols).rearrange("p t (n i) -> p n t i", i=RUN),
             )
 
-        def regroup_scalar_parts(c):
+        def regroup_pass_0(c):
             by_scalar[c] = scalar_pool.tile(
                 [P, 2 * CHUNK - GPSIMD_PIXELS, PACK], BF16, name="by_scalar", align_bytes=64
             )
-            whole_pass, rest = scalar_parts_of(c)
+            whole_pass, unused = scalar_parts_of(c)
             if c == 1:
                 copy_in_runs(nc.vector.tensor_copy, c, (0, slice(0, HALF), by_scalar[c][:, :HALF, :]))
                 copy_in_runs(nc.scalar.copy, c, (0, slice(HALF, CHUNK), by_scalar[c][:, HALF:CHUNK, :]))
             else:
                 copy_in_runs(nc.scalar.copy, c, whole_pass)
+
+        def regroup_rest(c):
+            unused, rest = scalar_parts_of(c)
             if c in through_tensor:
                 nc.scalar.copy(out=rest[2].rearrange("p n t -> p (n t)"), in_=through_tensor[c][:])
             else:
@@ -196,7 +204,10 @@ def tile_selfattentionconv2d_pa_t_kernel(tc, imgs, w_kv_words, w_kv_scales, out_
             )
 
         def multiply(c):
-            for r in range(ROW_TILES):
+            for g in range(PASSES):
+                for r in (0, 1):
+                    one_pass(c, r, g)
+            for r in (2, 3):
                 for g in range(PASSES):
                     one_pass(c, r, g)
 
@@ -210,6 +221,37 @@ def tile_selfattentionconv2d_pa_t_kernel(tc, imgs, w_kv_words, w_kv_scales, out_
                 return c, 1
             return c - c % CHUNKS_PER_STORE, CHUNKS_PER_STORE
 
+        def side(c, r, which):
+            return sums[(c, r)][:].rearrange("p (n e) -> p e n", e=2)[:, which, :]
+
+        def scalar_helps(c):
+            left[c] = left_pool.tile([P, HALF], F32, name="left")
+            nc.scalar.copy(out=left[c][:], in_=side(c, ROW_TILES - 1, 0))
+
+        def finish_helped(c):
+            first, chunks = store_of(c)
+            rows = row_max[c][:].rearrange("p (i d j) -> p d i j", d=2, j=POOLED_SIDE)
+            nc.vector.tensor_tensor(
+                out=pooled[(first, 1)][
+                    :, ROW_TILES_PER_OUTPUT - 1, (c - first) * POOLED_CHUNK : (c - first + 1) * POOLED_CHUNK
+                ].rearrange("p (i j) -> p i j", j=POOLED_SIDE),
+                in0=rows[:, 0],
+                in1=rows[:, 1],
+                op=mybir.AluOpType.max,
+            )
+            store(c, 1)
+
+        def store(c, which):
+            first, chunks = store_of(c)
+            if c == first + chunks - 1:
+                b, in_image = divmod(first, CHUNKS_PER_IMAGE)
+                nc.sync.dma_start(
+                    out=pooled_rows[which][
+                        b, :, :, in_image * POOLED_CHUNK : (in_image + chunks) * POOLED_CHUNK
+                    ],
+                    in_=pooled[(first, which)][:],
+                )
+
         def pool(c, row_tiles):
             first, chunks = store_of(c)
             for r in row_tiles:
@@ -218,6 +260,12 @@ def tile_selfattentionconv2d_pa_t_kernel(tc, imgs, w_kv_words, w_kv_scales, out_
                     pooled[(first, which)] = pooled_pool.tile(
                         [P, ROW_TILES_PER_OUTPUT, chunks * POOLED_CHUNK], F32, name="pooled"
                     )
+                if c in HELPED and r == ROW_TILES - 1:
+                    row_max[c] = row_max_pool.tile([P, HALF], F32, name="row_max")
+                    nc.vector.tensor_tensor(
+                        out=row_max[c][:], in0=side(c, r, 1), in1=left[c][:], op=mybir.AluOpType.max
+                    )
+                    continue
                 nc.vector.tensor_reduce(
                     out=pooled[(first, which)][
                         :, row_tile, (c - first) * POOLED_CHUNK : (c - first + 1) * POOLED_CHUNK
@@ -226,14 +274,8 @@ def tile_selfattentionconv2d_pa_t_kernel(tc, imgs, w_kv_words, w_kv_scales, out_
                     axis=mybir.AxisListType.XY,
                     op=mybir.AluOpType.max,
                 )
-                if c == first + chunks - 1 and row_tile == ROW_TILES_PER_OUTPUT - 1:
-                    b, in_image = divmod(first, CHUNKS_PER_IMAGE)
-                    nc.sync.dma_start(
-                        out=pooled_rows[which][
-                            b, :, :, in_image * POOLED_CHUNK : (in_image + chunks) * POOLED_CHUNK
-                        ],
-                        in_=pooled[(first, which)][:],
-                    )
+                if row_tile == ROW_TILES_PER_OUTPUT - 1:
+                    store(c, which)
 
         zeros = consts.tile([P, CHUNK], BF16)
         nc.vector.memset(zeros[:], 0.0)
@@ -262,13 +304,20 @@ def tile_selfattentionconv2d_pa_t_kernel(tc, imgs, w_kv_words, w_kv_scales, out_
                 quantise(0, passes=(g,))
                 for r in range(ROW_TILES):
                     one_pass(0, r, g)
-            regroup_scalar_parts(1)
+            regroup_pass_0(1)
+            regroup_rest(1)
             regroup_gpsimd_part(1)
             for c in range(CHUNKS):
                 if c + 2 < CHUNKS:
-                    regroup_scalar_parts(c + 2)
+                    regroup_pass_0(c + 2)
+                if c in HELPED:
+                    scalar_helps(c)
+                if c + 2 < CHUNKS:
+                    regroup_rest(c + 2)
                 before = ROW_TILES // 2
                 pool(c, range(0, before))
+                if c - 1 in HELPED:
+                    finish_helped(c - 1)
                 if c + 1 < CHUNKS:
                     quantise(c + 1)
                     multiply(c + 1)

@@ -33,6 +33,7 @@ CHUNKS_PER_STORE = 2
 STORES = CHUNKS // CHUNKS_PER_STORE
 
 FIRST_ON_TENSOR = 3
+TENSOR_PIXELS = 192
 HELPED = range(3, 15)
 WARM_UP = 6
 
@@ -134,7 +135,10 @@ def tile_selfattentionconv2d_pa_t_kernel(tc, imgs, w_kv_words, w_kv_scales, out_
         def regroup_rest(c):
             unused, rest = scalar_parts_of(c)
             if c in through_tensor:
-                nc.scalar.copy(out=rest[2].rearrange("p n t -> p (n t)"), in_=through_tensor[c][:])
+                nc.scalar.copy(
+                    out=rest[2][:, :TENSOR_PIXELS, :].rearrange("p n t -> p (n t)"), in_=through_tensor[c][:]
+                )
+                copy_in_runs(nc.scalar.copy, c, (1, slice(TENSOR_PIXELS, HALF), rest[2][:, TENSOR_PIXELS:, :]))
             else:
                 copy_in_runs(nc.scalar.copy, c, rest)
 
@@ -149,8 +153,8 @@ def tile_selfattentionconv2d_pa_t_kernel(tc, imgs, w_kv_words, w_kv_scales, out_
                 copy_in_runs(nc.vector.tensor_copy, 0, (1, slice(0, HALF), by_scalar[0][:, CHUNK:, :]))
 
         def regroup_on_tensor(c):
-            through_tensor[c] = regroup_psum.tile([P, HALF * PACK], BF16, name="regrouped_in_psum")
-            pixels = raw_pixels(c, 1, slice(0, HALF))
+            through_tensor[c] = regroup_psum.tile([P, TENSOR_PIXELS * PACK], BF16, name="regrouped_in_psum")
+            pixels = raw_pixels(c, 1, slice(0, TENSOR_PIXELS))
             for t in range(0, PACK, 2):
                 nc.tensor.matmul(
                     out=through_tensor[c][:].rearrange("p (n t) -> p t n", t=PACK)[:, t : t + 2, :],

@@ -24,7 +24,8 @@ ROW_TILES_PER_OUTPUT = ROW_TILES // 2
 
 CHUNK = 512
 HALF = CHUNK // 2
-GPSIMD_PIXELS = 256
+GPSIMD_PIXELS = 320
+GPSIMD_RUN = 2
 CHUNKS_PER_IMAGE = PIXELS // CHUNK
 CHUNKS = IMAGES * CHUNKS_PER_IMAGE
 POOLED_CHUNK = CHUNK // 4
@@ -33,7 +34,7 @@ CHUNKS_PER_STORE = 2
 STORES = CHUNKS // CHUNKS_PER_STORE
 
 FIRST_ON_TENSOR = 3
-TENSOR_PIXELS = 192
+TENSOR_PIXELS = CHUNK - GPSIMD_PIXELS
 HELPED = range(3, 15)
 WARM_UP = 6
 
@@ -98,7 +99,7 @@ def tile_selfattentionconv2d_pa_t_kernel(tc, imgs, w_kv_words, w_kv_scales, out_
             )
 
         def last_pixels(c):
-            return HALF if c == 0 else GPSIMD_PIXELS
+            return {0: HALF, 1: 192, 2: HALF}.get(c, GPSIMD_PIXELS)
 
         def in_allowed_widths(part):
             g, cols, regrouped = part
@@ -123,7 +124,7 @@ def tile_selfattentionconv2d_pa_t_kernel(tc, imgs, w_kv_words, w_kv_scales, out_
 
         def regroup_pass_0(c):
             by_scalar[c] = scalar_pool.tile(
-                [P, 2 * CHUNK - GPSIMD_PIXELS, PACK], BF16, name="by_scalar", align_bytes=64
+                [P, 2 * CHUNK - last_pixels(c), PACK], BF16, name="by_scalar", align_bytes=64
             )
             whole_pass, unused = scalar_parts_of(c)
             if c == 1:
@@ -136,9 +137,8 @@ def tile_selfattentionconv2d_pa_t_kernel(tc, imgs, w_kv_words, w_kv_scales, out_
             unused, rest = scalar_parts_of(c)
             if c in through_tensor:
                 nc.scalar.copy(
-                    out=rest[2][:, :TENSOR_PIXELS, :].rearrange("p n t -> p (n t)"), in_=through_tensor[c][:]
+                    out=rest[2].rearrange("p n t -> p (n t)"), in_=through_tensor[c][:]
                 )
-                copy_in_runs(nc.scalar.copy, c, (1, slice(TENSOR_PIXELS, HALF), rest[2][:, TENSOR_PIXELS:, :]))
             else:
                 copy_in_runs(nc.scalar.copy, c, rest)
 
@@ -167,8 +167,8 @@ def tile_selfattentionconv2d_pa_t_kernel(tc, imgs, w_kv_words, w_kv_scales, out_
         def copy_on_gpsimd(c, part):
             g, cols, regrouped = part
             nc.gpsimd.tensor_scalar(
-                out=regrouped,
-                in0=raw_pixels(c, g, cols).rearrange("p t n -> p n t"),
+                out=regrouped.rearrange("p (n i) t -> p n t i", i=GPSIMD_RUN),
+                in0=raw_pixels(c, g, cols).rearrange("p t (n i) -> p n t i", i=GPSIMD_RUN),
                 scalar1=1.0,
                 scalar2=0.0,
                 op0=mybir.AluOpType.mult,
@@ -176,7 +176,7 @@ def tile_selfattentionconv2d_pa_t_kernel(tc, imgs, w_kv_words, w_kv_scales, out_
             )
 
         def regroup_gpsimd_part(c):
-            by_gpsimd[c] = gpsimd_pool.tile([P, GPSIMD_PIXELS, PACK], BF16, name="by_gpsimd", align_bytes=64)
+            by_gpsimd[c] = gpsimd_pool.tile([P, last_pixels(c), PACK], BF16, name="by_gpsimd", align_bytes=64)
             copy_on_gpsimd(c, gpsimd_part_of(c))
 
         def quantise(c, passes=(0, 1)):
@@ -229,16 +229,17 @@ def tile_selfattentionconv2d_pa_t_kernel(tc, imgs, w_kv_words, w_kv_scales, out_
             return sums[(c, r)][:].rearrange("p (n e) -> p e n", e=2)[:, which, :]
 
         def scalar_helps(c):
-            left[c] = left_pool.tile([P, HALF], F32, name="left")
-            nc.scalar.copy(out=left[c][:], in_=side(c, ROW_TILES - 1, 0))
+            left[c] = left_pool.tile([P, ROW_TILES_PER_OUTPUT, HALF], F32, name="left")
+            for row_tile in range(ROW_TILES_PER_OUTPUT):
+                nc.scalar.copy(out=left[c][:, row_tile, :], in_=side(c, ROW_TILES_PER_OUTPUT + row_tile, 0))
 
         def finish_helped(c):
             first, chunks = store_of(c)
-            rows = row_max[c][:].rearrange("p (i d j) -> p d i j", d=2, j=POOLED_SIDE)
+            rows = row_max[c][:].rearrange("p r (i d j) -> p d r i j", d=2, j=POOLED_SIDE)
             nc.vector.tensor_tensor(
                 out=pooled[(first, 1)][
-                    :, ROW_TILES_PER_OUTPUT - 1, (c - first) * POOLED_CHUNK : (c - first + 1) * POOLED_CHUNK
-                ].rearrange("p (i j) -> p i j", j=POOLED_SIDE),
+                    :, :, (c - first) * POOLED_CHUNK : (c - first + 1) * POOLED_CHUNK
+                ].rearrange("p r (i j) -> p r i j", j=POOLED_SIDE),
                 in0=rows[:, 0],
                 in1=rows[:, 1],
                 op=mybir.AluOpType.max,
@@ -264,10 +265,14 @@ def tile_selfattentionconv2d_pa_t_kernel(tc, imgs, w_kv_words, w_kv_scales, out_
                     pooled[(first, which)] = pooled_pool.tile(
                         [P, ROW_TILES_PER_OUTPUT, chunks * POOLED_CHUNK], F32, name="pooled"
                     )
-                if c in HELPED and r == ROW_TILES - 1:
-                    row_max[c] = row_max_pool.tile([P, HALF], F32, name="row_max")
+                if c in HELPED and which == 1:
+                    if c not in row_max:
+                        row_max[c] = row_max_pool.tile([P, ROW_TILES_PER_OUTPUT, HALF], F32, name="row_max")
                     nc.vector.tensor_tensor(
-                        out=row_max[c][:], in0=side(c, r, 1), in1=left[c][:], op=mybir.AluOpType.max
+                        out=row_max[c][:, row_tile, :],
+                        in0=side(c, r, 1),
+                        in1=left[c][:, row_tile, :],
+                        op=mybir.AluOpType.max,
                     )
                     continue
                 nc.vector.tensor_reduce(
@@ -312,18 +317,18 @@ def tile_selfattentionconv2d_pa_t_kernel(tc, imgs, w_kv_words, w_kv_scales, out_
             regroup_rest(1)
             regroup_gpsimd_part(1)
             for c in range(CHUNKS):
-                if c + 2 < CHUNKS:
-                    regroup_pass_0(c + 2)
                 if c in HELPED:
                     scalar_helps(c)
                 if c + 2 < CHUNKS:
+                    regroup_pass_0(c + 2)
                     regroup_rest(c + 2)
                 before = ROW_TILES // 2
                 pool(c, range(0, before))
+                if c + 1 < CHUNKS:
+                    quantise(c + 1)
                 if c - 1 in HELPED:
                     finish_helped(c - 1)
                 if c + 1 < CHUNKS:
-                    quantise(c + 1)
                     multiply(c + 1)
                 if FIRST_ON_TENSOR <= c + 3 < CHUNKS:
                     regroup_on_tensor(c + 3)

from contextlib import ExitStack

import concourse.mybir as mybir
from concourse.masks import make_identity

BF16 = mybir.dt.bfloat16
F32 = mybir.dt.float32
I32 = mybir.dt.int32
U8 = mybir.dt.uint8
U32 = mybir.dt.uint32
FP8X4 = mybir.dt.float8_e4m3fn_x4
FP4X4 = mybir.dt.float4_e2m1fn_x4

P = 128
PACK = 4
IMAGES = 2
CHANNELS = 1024
SIDE = 64
PIXELS = SIDE * SIDE
OUT_ROWS = 512
PASSES = CHANNELS // (P * PACK)
ROW_TILES = OUT_ROWS // P
ROW_TILES_PER_OUTPUT = ROW_TILES // 2

CHUNK = 512
HALF = CHUNK // 2
GPSIMD_PIXELS = 320
GPSIMD_RUN = 2
CHUNKS_PER_IMAGE = PIXELS // CHUNK
CHUNKS = IMAGES * CHUNKS_PER_IMAGE
POOLED_CHUNK = CHUNK // 4
POOLED_SIDE = SIDE // 2
CHUNKS_PER_STORE = 2
STORES = CHUNKS // CHUNKS_PER_STORE

FIRST_ON_TENSOR = 3
TENSOR_PIXELS = CHUNK - GPSIMD_PIXELS
HELPED = range(3, 15)
WARM_UP = 6

RUN = 8

FLOPS = 2 * IMAGES * OUT_ROWS * CHANNELS * PIXELS

assert PASSES == 2


def tile_selfattentionconv2d_pa_t_kernel(tc, imgs, w_kv_words, w_kv_scales, out_0, out_1):
    nc = tc.nc
    channel_rows = imgs.rearrange("b (g p t) h w -> b g p t (h w)", g=PASSES, p=P, t=PACK)
    pooled_rows = [out.rearrange("b (r p) h w -> b p r (h w)", p=P) for out in (out_0, out_1)]

    with ExitStack() as ctx:
        consts = ctx.enter_context(tc.tile_pool(name="consts", bufs=1))
        raw_pool = ctx.enter_context(tc.tile_pool(name="raw", bufs=CHUNKS * PASSES + 1))
        scalar_pool = ctx.enter_context(tc.tile_pool(name="by_scalar", bufs=3))
        gpsimd_pool = ctx.enter_context(tc.tile_pool(name="by_gpsimd", bufs=1))
        quantised_pool = ctx.enter_context(tc.tile_pool(name="quantised", bufs=3))
        pooled_pool = ctx.enter_context(tc.tile_pool(name="pooled", bufs=2 * (STORES + 1)))
        left_pool = ctx.enter_context(tc.tile_pool(name="left", bufs=2))
        row_max_pool = ctx.enter_context(tc.tile_pool(name="row_max", bufs=2))
        psum = ctx.enter_context(tc.psum_pool(name="psum", bufs=ROW_TILES + ROW_TILES // 2))
        regroup_psum = ctx.enter_context(tc.psum_pool(name="regroup_psum", bufs=2))

        raw = {}
        by_scalar = {}
        by_gpsimd = {}
        through_tensor = {}
        x_codes = {}
        x_scales = {}
        sums = {}
        left = {}
        row_max = {}
        pooled = {}

        def load(c):
            b, in_image = divmod(c, CHUNKS_PER_IMAGE)
            for g in range(PASSES):
                width = load_width(c, g)
                for first in range(0, CHUNK, width):
                    raw[(c, g, first)] = raw_pool.tile([P, PACK, width], BF16, name="raw")
                    nc.sync.dma_start(
                        out=raw[(c, g, first)][:],
                        in_=channel_rows[b, g, :, :, in_image * CHUNK + first : in_image * CHUNK + first + width],
                    )

        def load_width(c, g):
            return HALF if (c, g) == (0, 0) else CHUNK

        def raw_pixels(c, g, cols):
            first = cols.start - cols.start % load_width(c, g)
            assert cols.stop <= first + load_width(c, g)
            return raw[(c, g, first)][:, :, cols.start - first : cols.stop - first]

        def scalar_parts_of(c):
            return (
                (0, slice(0, CHUNK), by_scalar[c][:, :CHUNK, :]),
                (1, slice(0, CHUNK - last_pixels(c)), by_scalar[c][:, CHUNK:, :]),
            )

        def last_pixels(c):
            return {0: HALF, 1: 192, 2: HALF}.get(c, GPSIMD_PIXELS)

        def in_allowed_widths(part):
            g, cols, regrouped = part
            pieces = []
            at = cols.start
            for width in (512, 256, 128, 64):
                if cols.stop - at >= width:
                    pieces.append((g, slice(at, at + width), regrouped[:, at - cols.start : at - cols.start + width, :]))
                    at += width
            assert at == cols.stop
            return pieces

        def gpsimd_part_of(c):
            return (1, slice(CHUNK - last_pixels(c), CHUNK), by_gpsimd[c][:])

        def copy_in_runs(copy, c, part):
            g, cols, regrouped = part
            copy(
                out=regrouped.rearrange("p (n i) t -> p n t i", i=RUN),
                in_=raw_pixels(c, g, cols).rearrange("p t (n i) -> p n t i", i=RUN),
            )

        def regroup_pass_0(c):
            by_scalar[c] = scalar_pool.tile(
                [P, 2 * CHUNK - last_pixels(c), PACK], BF16, name="by_scalar", align_bytes=64
            )
            whole_pass, unused = scalar_parts_of(c)
            if c == 1:
                copy_in_runs(nc.vector.tensor_copy, c, (0, slice(0, HALF), by_scalar[c][:, :HALF, :]))
                copy_in_runs(nc.scalar.copy, c, (0, slice(HALF, CHUNK), by_scalar[c][:, HALF:CHUNK, :]))
            else:
                copy_in_runs(nc.scalar.copy, c, whole_pass)

        def regroup_rest(c):
            unused, rest = scalar_parts_of(c)
            if c in through_tensor:
                nc.scalar.copy(
                    out=rest[2].rearrange("p n t -> p (n t)"), in_=through_tensor[c][:]
                )
            else:
                copy_in_runs(nc.scalar.copy, c, rest)

        def regroup_first_chunk(g):
            if g == 0:
                by_scalar[0] = scalar_pool.tile([P, CHUNK + HALF, PACK], BF16, name="by_scalar", align_bytes=64)
                by_gpsimd[0] = gpsimd_pool.tile([P, HALF, PACK], BF16, name="by_gpsimd", align_bytes=64)
                copy_in_runs(nc.scalar.copy, 0, gpsimd_part_of(0))
                copy_in_runs(nc.vector.tensor_copy, 0, (0, slice(0, HALF), by_scalar[0][:, :HALF, :]))
                copy_in_runs(nc.vector.tensor_copy, 0, (0, slice(HALF, CHUNK), by_scalar[0][:, HALF:CHUNK, :]))
            else:
                copy_in_runs(nc.vector.tensor_copy, 0, (1, slice(0, HALF), by_scalar[0][:, CHUNK:, :]))

        def regroup_on_tensor(c):
            through_tensor[c] = regroup_psum.tile([P, TENSOR_PIXELS * PACK], BF16, name="regrouped_in_psum")
            pixels = raw_pixels(c, 1, slice(0, TENSOR_PIXELS))
            for t in range(0, PACK, 2):
                nc.tensor.matmul(
                    out=through_tensor[c][:].rearrange("p (n t) -> p t n", t=PACK)[:, t : t + 2, :],
                    lhsT=identity[:],
                    rhs=pixels[:, t : t + 2, :],
                    start=True,
                    stop=True,
                )

        def copy_on_gpsimd(c, part):
            g, cols, regrouped = part
            nc.gpsimd.tensor_scalar(
                out=regrouped.rearrange("p (n i) t -> p n t i", i=GPSIMD_RUN),
                in0=raw_pixels(c, g, cols).rearrange("p t (n i) -> p n t i", i=GPSIMD_RUN),
                scalar1=1.0,
                scalar2=0.0,
                op0=mybir.AluOpType.mult,
                op1=mybir.AluOpType.add,
            )

        def regroup_gpsimd_part(c):
            by_gpsimd[c] = gpsimd_pool.tile([P, last_pixels(c), PACK], BF16, name="by_gpsimd", align_bytes=64)
            copy_on_gpsimd(c, gpsimd_part_of(c))

        def quantise(c, passes=(0, 1)):
            if c not in x_codes:
                x_codes[c] = quantised_pool.tile([P, PASSES, CHUNK], U32, name="x_codes", align_bytes=64)
                x_scales[c] = quantised_pool.tile([P, PASSES, CHUNK], U8, name="x_scales", align_bytes=64)
            pieces = []
            for part in scalar_parts_of(c) + (gpsimd_part_of(c),):
                pieces.extend(in_allowed_widths(part))
            for g, cols, regrouped in pieces:
                if g in passes:
                    nc.vector.quantize_mx(
                        out=x_codes[c][:, g, cols].bitcast(FP8X4),
                        scales=x_scales[c][:, g, cols],
                        in_=regrouped.rearrange("p n t -> p (n t)"),
                    )

        def one_pass(c, r, g):
            if g == 0:
                sums[(c, r)] = psum.tile([P, CHUNK], F32, name="sums")
            nc.tensor.matmul_mx(
                out=sums[(c, r)][:],
                lhsT=w_words[:, g, 2 * P * r : 2 * P * (r + 1)].bitcast(FP4X4),
                lhsT_scale=w_scales[:, g, P * r : P * (r + 1)],
                rhs=x_codes[c][:, g, :].bitcast(FP8X4),
                rhs_scale=x_scales[c][:, g, :],
                start=(g == 0),
                stop=(g == PASSES - 1),
            )

        def multiply(c):
            for g in range(PASSES):
                for r in (0, 1):
                    one_pass(c, r, g)
            for r in (2, 3):
                for g in range(PASSES):
                    one_pass(c, r, g)

        def warm_up():
            unread = psum.tile([P, CHUNK], F32, name="sums")
            for i in range(WARM_UP):
                nc.tensor.matmul(out=unread[:], lhsT=zeros[:, :P], rhs=zeros[:], start=True, stop=True)

        def store_of(c):
            if c >= CHUNKS - CHUNKS_PER_STORE:
                return c, 1
            return c - c % CHUNKS_PER_STORE, CHUNKS_PER_STORE

        def side(c, r, which):
            return sums[(c, r)][:].rearrange("p (n e) -> p e n", e=2)[:, which, :]

        def scalar_helps(c):
            left[c] = left_pool.tile([P, ROW_TILES_PER_OUTPUT, HALF], F32, name="left")
            for row_tile in range(ROW_TILES_PER_OUTPUT):
                nc.scalar.copy(out=left[c][:, row_tile, :], in_=side(c, ROW_TILES_PER_OUTPUT + row_tile, 0))

        def finish_helped(c):
            first, chunks = store_of(c)
            rows = row_max[c][:].rearrange("p r (i d j) -> p d r i j", d=2, j=POOLED_SIDE)
            nc.vector.tensor_tensor(
                out=pooled[(first, 1)][
                    :, :, (c - first) * POOLED_CHUNK : (c - first + 1) * POOLED_CHUNK
                ].rearrange("p r (i j) -> p r i j", j=POOLED_SIDE),
                in0=rows[:, 0],
                in1=rows[:, 1],
                op=mybir.AluOpType.max,
            )
            store(c, 1)

        def store(c, which):
            first, chunks = store_of(c)
            if c == first + chunks - 1:
                b, in_image = divmod(first, CHUNKS_PER_IMAGE)
                nc.sync.dma_start(
                    out=pooled_rows[which][
                        b, :, :, in_image * POOLED_CHUNK : (in_image + chunks) * POOLED_CHUNK
                    ],
                    in_=pooled[(first, which)][:],
                )

        def pool(c, row_tiles):
            first, chunks = store_of(c)
            for r in row_tiles:
                which, row_tile = divmod(r, ROW_TILES_PER_OUTPUT)
                if (first, which) not in pooled:
                    pooled[(first, which)] = pooled_pool.tile(
                        [P, ROW_TILES_PER_OUTPUT, chunks * POOLED_CHUNK], F32, name="pooled"
                    )
                if c in HELPED and which == 1:
                    if c not in row_max:
                        row_max[c] = row_max_pool.tile([P, ROW_TILES_PER_OUTPUT, HALF], F32, name="row_max")
                    nc.vector.tensor_tensor(
                        out=row_max[c][:, row_tile, :],
                        in0=side(c, r, 1),
                        in1=left[c][:, row_tile, :],
                        op=mybir.AluOpType.max,
                    )
                    continue
                nc.vector.tensor_reduce(
                    out=pooled[(first, which)][
                        :, row_tile, (c - first) * POOLED_CHUNK : (c - first + 1) * POOLED_CHUNK
                    ].rearrange("p (i j) -> p i j", j=POOLED_SIDE),
                    in_=sums[(c, r)][:].rearrange("p (i di j dj) -> p i j di dj", di=2, j=POOLED_SIDE, dj=2),
                    axis=mybir.AxisListType.XY,
                    op=mybir.AluOpType.max,
                )
                if row_tile == ROW_TILES_PER_OUTPUT - 1:
                    store(c, which)

        zeros = consts.tile([P, CHUNK], BF16)
        nc.vector.memset(zeros[:], 0.0)
        identity = consts.tile([P, P], BF16)
        make_identity(nc, identity[:])

        load(0)

        w_words = consts.tile([P, PASSES, 2 * OUT_ROWS], U8, align_bytes=64)
        nc.sync.dma_start(out=w_words[:].bitcast(I32), in_=w_kv_words.bitcast(I32).rearrange("g p n -> p g n"))
        w_scales = consts.tile([P, PASSES, OUT_ROWS], U8, align_bytes=64)
        nc.vector.memset(w_scales[:].bitcast(I32), 0)
        for quadrant in range(4):
            nc.sync.dma_start(
                out=w_scales[32 * quadrant : 32 * quadrant + 4, :, :].bitcast(I32),
                in_=w_kv_scales.bitcast(I32)[:, 4 * quadrant : 4 * quadrant + 4, :].rearrange("g q n -> q g n"),
            )

        for c in range(1, CHUNKS):
            load(c)

        with tc.manual_schedule():
            warm_up()
            for g in range(PASSES):
                regroup_first_chunk(g)
                quantise(0, passes=(g,))
                for r in range(ROW_TILES):
                    one_pass(0, r, g)
            regroup_pass_0(1)
            regroup_rest(1)
            regroup_gpsimd_part(1)
            for c in range(CHUNKS):
                if c in HELPED:
                    scalar_helps(c)
                if c + 2 < CHUNKS:
                    regroup_pass_0(c + 2)
                    regroup_rest(c + 2)
                before = ROW_TILES // 2
                pool(c, range(0, before))
                if c + 1 < CHUNKS:
                    quantise(c + 1)
                if c - 1 in HELPED:
                    finish_helped(c - 1)
                if c + 1 < CHUNKS:
                    multiply(c + 1)
                if FIRST_ON_TENSOR <= c + 3 < CHUNKS:
                    regroup_on_tensor(c + 3)
                if c + 2 < CHUNKS:
                    regroup_gpsimd_part(c + 2)
                pool(c, range(before, ROW_TILES))
